import numpy as np
import ml_dtypes


def mxq(x, axis, fmt="e4m3"):
    dtype, down = {"e4m3": (ml_dtypes.float8_e4m3fn, 7), "e5m2": (ml_dtypes.float8_e5m2, 14)}[fmt]
    v = np.moveaxis(np.asarray(x, np.float32).astype(ml_dtypes.bfloat16).astype(np.float64), axis, -1)
    blocks = v.reshape(v.shape[:-1] + (-1, 32))
    amax = np.abs(blocks).max(-1, keepdims=True)
    byte = np.maximum(np.where(amax > 0, np.frexp(amax)[1] - 1 + 127, 0) - down, 1)
    scale = np.exp2(byte - 127.0)
    codes = (blocks / scale).astype(np.float32).astype(dtype).astype(np.float64)
    return np.moveaxis((codes * scale).reshape(v.shape), -1, axis)


WIDE = False


def mx_kscale(k):
    if not WIDE:
        return np.ones(k)
    levels = np.array([10, -10, 5, -5, 0])
    a = np.random.permutation(np.resize(levels, k // 512 * 4)).reshape(k // 512, 4)
    idx = np.arange(k)
    return np.exp2(a[idx // 512, idx % 128 // 32])


BF16 = ml_dtypes.bfloat16


def bf(x):
    return np.asarray(x, np.float32).astype(BF16)


def f64(x):
    return np.asarray(x).astype(np.float64)


E2M1 = np.array([0.0, 0.5, 1.0, 1.5, 2.0, 3.0, 4.0, 6.0, -0.0, -0.5, -1.0, -1.5, -2.0, -3.0, -4.0, -6.0])


def pack_weight(w, fmt):
    k, n = w.shape
    w = f64(bf(w)).reshape(k // 32, 32, n)
    amax = np.abs(w).max(1)
    if fmt == "e4m3":
        byte = np.frexp(amax)[1] - 1 + 127 - 7
    else:
        mant, ex = np.frexp(amax / 6.0)
        byte = np.where(mant > 0.5, ex, ex - 1) + 127
    byte = np.clip(np.where(amax > 0, byte, 1), 1, 254)
    scaled = (w * np.exp2(127.0 - byte)[:, None, :]).reshape(k, n).astype(np.float32)
    by_word = np.ascontiguousarray(scaled.reshape(k // 512, 128, 4, n).transpose(0, 1, 3, 2))
    if fmt == "e4m3":
        words = by_word.astype(ml_dtypes.float8_e4m3fn).view(np.uint8)
    else:
        c = by_word.astype(ml_dtypes.float4_e2m1fn).view(np.uint8) & 0xF
        words = c[..., 0::2] | (c[..., 1::2] << 4)
    return np.ascontiguousarray(words), np.ascontiguousarray(byte.astype(np.uint8).reshape(k // 512, 16, n))


def unpack_weight(words, scales, fmt):
    g, p, n, _ = words.shape
    if fmt == "e4m3":
        vals = np.ascontiguousarray(words).view(ml_dtypes.float8_e4m3fn).astype(np.float64)
    else:
        nib = np.empty((g, p, n, 4), np.uint8)
        nib[..., 0::2] = words & 0xF
        nib[..., 1::2] = words >> 4
        vals = E2M1[nib]
    vals = vals * np.repeat(np.exp2(scales.astype(np.float64) - 127.0), 8, axis=1)[..., None]
    return vals.transpose(0, 1, 3, 2).reshape(g * 512, n)


M, K, N = 128, 4096, 4096
TINY = 1e-15
EPS = 1e-6
C = 1.0
S = 1.0 / np.sqrt(C)
SQRTC = np.sqrt(C)


def _asinh(t):
    return np.log(t + np.sqrt(t * t + 1.0))


def _sinh(t):
    return 0.5 * (np.exp(t) - np.exp(-t))


def _norm(p):
    return np.sqrt(np.sum(p * p, axis=-1, keepdims=True))


def _sinhc(z):
    y = _sinh(z) / np.maximum(z, EPS)
    y0 = 1.0 + z * z / 6.0
    return np.where(np.abs(z) < EPS, y0, y)


def _beta(x):
    denom = np.sqrt(1.0 + C * np.sum(x * x, axis=-1, keepdims=True))
    return 1.0 / np.maximum(denom, TINY)


def _log0(y):
    s = _norm(y)
    coef = _asinh(s / S) / np.maximum(s / S, EPS)
    return coef * y


def _exp0(v):
    r = _norm(v)
    coef = _sinh(r / S) / np.maximum(r / S, EPS)
    return coef * v


def _proj_tan0(v, max_norm=20.0):
    r = np.maximum(_norm(v), EPS)
    return np.minimum(max_norm / r, 1.0) * v


def _pt_0_to_y(y, v):
    b = _beta(y)
    coef = C * b / (1.0 + b)
    dot = np.sum(y * v, axis=-1, keepdims=True)
    return v + coef * dot * y


def _gyro_add(x, y):
    b_x = _beta(x)
    b_y = _beta(y)
    s2 = S * S
    xy = np.sum(x * y, axis=-1, keepdims=True)
    coef = b_x / (1.0 + b_x) * (xy / s2) + (1.0 - b_y) / b_y
    return x + y + coef * x


def _exp_map(x, v):
    s2 = S * S
    x_norm2 = np.sum(x * x, axis=-1, keepdims=True)
    v_norm2 = np.sum(v * v, axis=-1, keepdims=True)
    dot_x_v = np.sum(x * v, axis=-1, keepdims=True)
    g_pvv = np.maximum(v_norm2 - dot_x_v * dot_x_v / (s2 + x_norm2), TINY)
    r_g = np.sqrt(g_pvv)
    b_x = _beta(x)
    coef1 = b_x / (1.0 + b_x)
    coef2 = -(C * b_x ** 3) / np.maximum(1.0 + b_x, TINY) ** 2
    dpi_v = coef1 * v + coef2 * dot_x_v * x
    lambda_x = (1.0 + b_x) / np.maximum(b_x, TINY)
    z_arg = np.clip(SQRTC * r_g, -20.0, 20.0)
    w = lambda_x * _sinhc(z_arg) * dpi_v
    return _gyro_add(x, w)


def setup_inputs():
    xn, un, bn = 3.0, 2.0, 2.0
    ax, aw, ab = 0.5, 2.0, 0.75
    s = mx_kscale(K)
    s = s / np.sqrt(np.mean(s * s))
    xs = xn / np.sqrt(K * (1.0 + ax * ax))
    ws = un / (_asinh(xn) * np.sqrt(N * (1.0 + ax * ax + ax * ax * aw * aw) / (1.0 + ax * ax)))
    bs = bn / np.sqrt(N * (1.0 + ab * ab))
    x = bf((np.random.standard_normal((M, K)) + ax) * xs * s)
    w_nk = (np.random.standard_normal((N, K)) + aw / np.sqrt(K)) * ws / s
    words, scales = pack_weight(np.ascontiguousarray(w_nk.T), "e4m3")
    b = bf((np.random.standard_normal(N) + ab) * bs)
    return {"x": x, "W_words": words, "W_scales": scales, "b": b}


def reference(x, W_words, W_scales, b):
    x, b = f64(x), f64(b)
    v = _log0(x)
    u = mxq(v, 1, "e4m3") @ unpack_weight(W_words, W_scales, "e4m3")
    u = _proj_tan0(u)
    y = _exp0(u)
    bt = _pt_0_to_y(y, b)
    return _exp_map(y, bt)

@@ -1,0 +1,290 @@
+from contextlib import ExitStack
+
+import concourse.masks as masks
+import concourse.mybir as mybir
+
+F32 = mybir.dt.float32
+BF16 = mybir.dt.bfloat16
+I32 = mybir.dt.int32
+U32 = mybir.dt.uint32
+U8 = mybir.dt.uint8
+FP8X4 = mybir.dt.float8_e4m3fn_x4
+ALU = mybir.AluOpType
+ACT = mybir.ActivationFunctionType
+AX = mybir.AxisListType
+
+P = 128
+M, K, N = 128, 4096, 4096
+K_PASS = 512
+GROUPS = K // K_PASS
+BANK = 512
+BANKS = N // BANK
+FLOPS = 2 * M * K * N
+
+
+def tile_pvfc_w_kernel(tc, x, W_words, W_scales, b, out):
+    nc = tc.nc
+    with ExitStack() as ctx:
+        ctx.enter_context(tc.manual_schedule())
+        big = ctx.enter_context(tc.tile_pool(name="big", bufs=1))
+        sm = ctx.enter_context(tc.tile_pool(name="sm", bufs=1))
+        psum = ctx.enter_context(tc.psum_pool(name="psum", bufs=1))
+
+        def col(name, width=1):
+            return sm.tile([P, width], F32, name=name)
+
+        def ts2(o, i, s1, s2, op0, op1):
+            nc.vector.tensor_scalar(out=o, in0=i, scalar1=s1, scalar2=s2, op0=op0, op1=op1)
+
+        def ts1(o, i, s1, op0):
+            nc.vector.tensor_scalar(out=o, in0=i, scalar1=s1, scalar2=None, op0=op0)
+
+        def stt(o, i0, s, i1, op0, op1):
+            nc.vector.scalar_tensor_tensor(out=o, in0=i0, scalar=s, in1=i1, op0=op0, op1=op1)
+
+        def tt(o, i0, i1, op):
+            nc.vector.tensor_tensor(out=o, in0=i0, in1=i1, op=op)
+
+        x_sb = big.tile([P, K], BF16, name="x_sb")
+        brow = big.tile([P, N], BF16, name="brow")
+        b_bc = big.tile([P, N], BF16, name="b_bc")
+        t_sb = big.tile([P, N], F32, name="t_sb")
+        o_sb = big.tile([P, N], F32, name="o_sb")
+        grouped = big.tile([P, GROUPS, K_PASS], BF16, name="grouped", align_bytes=64)
+        v_codes = big.tile([P, GROUPS * P], U32, name="v_codes", align_bytes=64)
+        v_scales = big.tile([P, GROUPS * P], U8, name="v_scales", align_bytes=64)
+        planes = [big.tile([P, N], U8, name="planes%d" % h, align_bytes=64) for h in range(2)]
+        w = [big.tile([P, N], U32, name="w%d" % g, align_bytes=64) for g in range(GROUPS)]
+        junk_s = big.tile([P, BANK], F32, name="junk_s")
+        junk_v = big.tile([P, BANK], F32, name="junk_v")
+        ident = big.tile([P, P], F32, name="ident")
+        ones_bf = big.tile([P, P], BF16, name="ones_bf")
+        ones_f = big.tile([P, P], F32, name="ones_f")
+        rep = big.tile([P, P], F32, name="rep")
+        coef_bc = big.tile([P, P], F32, name="coef_bc")
+
+        pw3 = col("pw3", 3)
+        hi2 = col("hi2", 2)
+        one1 = col("one1")
+        scr1 = col("scr1")
+
+        nc.vector.memset(one1[:], 1.0)
+        nc.scalar.activation(out=scr1[:], in_=one1[:], func=ACT.Ln)
+        masks.make_identity(nc, ident[:])
+        for h in range(2):
+            nc.vector.memset(planes[h][:].bitcast(I32), 0)
+        nc.vector.memset(brow[:].bitcast(I32), 0)
+        nc.vector.memset(pw3[:, 0:2], 0.5)
+        nc.vector.memset(pw3[:, 2:3], -0.5)
+        nc.vector.memset(hi2[:, 0:1], 400.0)
+        nc.vector.memset(hi2[:, 1:2], 3.0e38)
+        nc.vector.memset(ones_bf[:], 1.0)
+        nc.vector.memset(ones_f[:], 1.0)
+
+        half = K // 2
+        for h in range(2):
+            nc.sync.dma_start(out=x_sb[:, h * half:(h + 1) * half], in_=x[:, h * half:(h + 1) * half])
+        nc.scalar.dma_start(out=brow[0:1, :], in_=b.unsqueeze(0))
+        for h in range(2):
+            for q in range(4):
+                nc.sync.dma_start(
+                    out=planes[h][32 * q:32 * q + 16, :].bitcast(I32),
+                    in_=W_scales[4 * h:4 * h + 4, 4 * q:4 * q + 4, :].bitcast(I32),
+                )
+        chunks = [(g, 0, N) for g in range(GROUPS - 1)]
+        chunks.extend([(GROUPS - 1, j * BANK, (j + 1) * BANK) for j in range(BANKS)])
+        for g, n0, n1 in chunks:
+            nc.sync.dma_start(
+                out=w[g][:, n0:n1].bitcast(I32),
+                in_=W_words[g, :, n0:n1, :].rearrange("p n t -> p (n t)").bitcast(I32),
+            )
+
+        ssv = col("ssv")
+        sss = col("sss")
+        nc.vector.scalar_tensor_tensor(
+            out=o_sb[:, 0:half], in0=x_sb[:, 0:half], scalar=1.0, in1=x_sb[:, 0:half],
+            op0=ALU.mult, op1=ALU.mult, accum_out=ssv[:],
+        )
+        nc.scalar.activation(out=o_sb[:, half:K], in_=x_sb[:, half:K], func=ACT.Square, accum_out=sss[:])
+
+        xw = x_sb[:].bitcast(F32)
+        xt = []
+        for i in range(4):
+            xt_i = psum.tile([P, 4, P], F32, name="xt%d" % i, tag="bk%d" % (4 + i))
+            xt.append(xt_i)
+            for gg in range(2):
+                for u in range(2):
+                    g = 2 * i + gg
+                    nc.tensor.transpose(xt_i[:, 2 * gg + u, :], xw[:, 256 * g + u:256 * (g + 1):2], ident[:])
+
+        for i in range(4):
+            b_ps = psum.tile([P, 2 * BANK], BF16, name="b_ps%d" % i, tag="bk%d" % i)
+            for c in range(2):
+                n0 = (2 * i + c) * BANK
+                nc.tensor.matmul(b_ps[:, c * BANK:(c + 1) * BANK], lhsT=ones_bf[:], rhs=brow[:, n0:n0 + BANK],
+                                 start=True, stop=True)
+            nc.scalar.copy(out=b_bc[:, 2 * i * BANK:(2 * i + 2) * BANK], in_=b_ps[:])
+            if i == 0:
+                ss3 = col("ss3", 3)
+                sq3 = col("sq3", 3)
+                lnv = col("lnv")
+                pa = col("pa")
+                mkx = col("mkx")
+                dx = col("dx")
+                lsel = col("lsel")
+                coef = col("coef")
+                tt(ss3[:, 0:1], ssv[:], sss[:], ALU.add)
+                ts1(ss3[:, 1:2], ss3[:, 0:1], 1.0, ALU.add)
+                ts1(ss3[:, 2:3], ss3[:, 0:1], 1e-12, ALU.max)
+                nc.gpsimd.tensor_tensor(out=sq3[:], in0=ss3[:], in1=pw3[:], op=ALU.pow)
+                nc.scalar.activation(out=lnv[:], in_=sq3[:, 0:1], func=ACT.Ln, bias=sq3[:, 1:2], scale=1.0)
+                ss = ss3[:, 0:1]
+                ts2(pa[:], ss, 35.0 / 1152.0, -5.0 / 112.0, ALU.mult, ALU.add)
+                ts2(pa[:], pa[:], ss, 3.0 / 40.0, ALU.mult, ALU.add)
+                ts2(pa[:], pa[:], ss, -1.0 / 6.0, ALU.mult, ALU.add)
+                ts2(pa[:], pa[:], ss, 1.0, ALU.mult, ALU.add)
+                ts1(mkx[:], ss, 1.0 / 64.0, ALU.is_lt)
+                stt(dx[:], pa[:], sq3[:, 0:1], lnv[:], ALU.mult, ALU.subtract)
+                stt(lsel[:], dx[:], mkx[:], lnv[:], ALU.mult, ALU.add)
+                tt(coef[:], lsel[:], sq3[:, 2:3], ALU.mult)
+                ts1(rep[:], ones_f[:], coef[:], ALU.mult)
+
+        ct = psum.tile([P, P], F32, name="ct", tag="bk0")
+        nc.tensor.transpose(ct[:], rep[:], ident[:])
+        nc.vector.tensor_copy(out=coef_bc[:], in_=ct[:])
+
+        def scale_group(g):
+            src = xt[g // 2][:, 2 * (g % 2):2 * (g % 2) + 2, :].bitcast(BF16)
+            tt(
+                grouped[:, g, :].rearrange("p (m u e) -> p m u e", u=2, e=2),
+                src.rearrange("p u (m e) -> p m u e", e=2),
+                coef_bc[:].unsqueeze(2).unsqueeze(3).to_broadcast([P, P, 2, 2]),
+                ALU.mult,
+            )
+
+        def quantise_pair(i):
+            nc.vector.quantize_mx(
+                out=v_codes[:, 2 * i * P:(2 * i + 2) * P].bitcast(FP8X4),
+                scales=v_scales[:, 2 * i * P:(2 * i + 2) * P],
+                in_=grouped[:, 2 * i:2 * i + 2, :].rearrange("p g c -> p (g c)"),
+            )
+
+        scale_group(0)
+        scale_group(1)
+        for i in range(3):
+            scale_group(2 * i + 2)
+            quantise_pair(i)
+            scale_group(2 * i + 3)
+        quantise_pair(3)
+
+        bb = col("bb")
+        bz2 = col("bz2", 2)
+        zz = col("zz", 2)
+        ez = col("ez")
+        ezi = col("ezi")
+        pz = col("pz")
+        mkz = col("mkz")
+        qz = col("qz")
+        bigz = col("bigz")
+        sc = col("sc")
+        g2 = col("g2")
+        gw = col("gw")
+        nc.scalar.activation(out=t_sb[:], in_=b_bc[:], func=ACT.Square, accum_out=bb[:])
+        ts2(bz2[:], bb[:, 0:1].to_broadcast([P, 2]), 1e-15, 400.0, ALU.max, ALU.min)
+        nc.gpsimd.tensor_tensor(out=zz[:], in0=bz2[:], in1=pw3[:, 1:3], op=ALU.pow)
+        nc.scalar.activation(out=ez[:], in_=zz[:, 0:1], func=ACT.Exp)
+        nc.scalar.activation(out=ezi[:], in_=zz[:, 0:1], func=ACT.Exp, scale=-1.0)
+        bz = bz2[:, 0:1]
+        ts2(pz[:], bz, 1.0 / 5040.0, 1.0 / 120.0, ALU.mult, ALU.add)
+        ts2(pz[:], pz[:], bz, 1.0 / 6.0, ALU.mult, ALU.add)
+        ts2(pz[:], pz[:], bz, 1.0, ALU.mult, ALU.add)
+        ts1(mkz[:], bz, 1.0 / 16.0, ALU.is_lt)
+        ts2(qz[:], mkz[:], -0.5, 0.5, ALU.mult, ALU.add)
+        tt(qz[:], qz[:], zz[:, 1:2], ALU.mult)
+        stt(bigz[:], ez[:], ezi[:], qz[:], ALU.subtract, ALU.mult)
+        stt(sc[:], pz[:], mkz[:], bigz[:], ALU.mult, ALU.add)
+        tt(g2[:], sc[:], sc[:], ALU.mult)
+        ts2(g2[:], g2[:], bb[:], 1.0, ALU.mult, ALU.add)
+        nc.gpsimd.tensor_tensor(out=gw[:], in0=g2[:], in1=pw3[:, 0:1], op=ALU.pow)
+        nc.scalar.activation(out=t_sb[:], in_=b_bc[:], func=ACT.Copy, scale=sc[:])
+
+        acc = [None] * BANKS
+
+        def mx_pass(g, j):
+            k_off = 4 * (g % 4)
+            nc.tensor.matmul_mx(
+                out=acc[j][:],
+                lhsT=v_codes[:, g * P:(g + 1) * P].bitcast(FP8X4),
+                lhsT_scale=v_scales[:, g * P:(g + 1) * P],
+                rhs=w[g][:, j * BANK:(j + 1) * BANK].bitcast(FP8X4),
+                rhs_scale=planes[g // 4][k_off:P, j * BANK:(j + 1) * BANK],
+                start=(g == 0),
+                stop=(g == GROUPS - 1),
+            )
+
+        for j in range(BANKS):
+            acc[j] = psum.tile([P, BANK], F32, name="acc%d" % j, tag="bk%d" % j)
+            mx_pass(0, j)
+        for g in range(1, GROUPS - 1):
+            for j in range(BANKS):
+                mx_pass(g, j)
+
+        s1 = col("s1", BANKS)
+        s2 = col("s2", BANKS)
+
+        def dot_t(j):
+            nc.vector.scalar_tensor_tensor(
+                out=junk_v[:], in0=acc[j][:], scalar=1.0, in1=t_sb[:, j * BANK:(j + 1) * BANK],
+                op0=ALU.mult, op1=ALU.mult, accum_out=s2[:, j:j + 1],
+            )
+
+        for j in range(BANKS):
+            mx_pass(GROUPS - 1, j)
+            nc.scalar.activation(out=junk_s[:], in_=acc[j][:], func=ACT.Square, accum_out=s1[:, j:j + 1])
+            if j < BANKS - 1:
+                dot_t(j)
+
+        nn = col("nn", 2)
+        rq = col("rq", 2)
+        pr = col("pr")
+        mkr = col("mkr")
+        qsel = col("qsel")
+        qc = col("qc")
+        d0 = col("d0")
+        w1 = col("w1")
+        small = col("small")
+        th = col("th")
+        er = col("er")
+        eri = col("eri")
+        tf = col("tf")
+        smt = col("smt")
+        sh = col("sh")
+        fac = col("fac")
+        nc.vector.tensor_reduce(out=nn[:], in_=s1[:].unsqueeze(1).to_broadcast([P, 2, BANKS]), axis=AX.X, op=ALU.add)
+        tt(nn[:], nn[:], hi2[:], ALU.min)
+        nc.gpsimd.tensor_tensor(out=rq[:], in0=nn[:], in1=pw3[:, 1:3], op=ALU.pow)
+        nc.scalar.activation(out=th[:], in_=rq[:, 0:1], func=ACT.Tanh, scale=0.5)
+        nc.scalar.activation(out=eri[:], in_=rq[:, 0:1], func=ACT.Exp, scale=-1.0)
+        nc.scalar.activation(out=er[:], in_=rq[:, 0:1], func=ACT.Exp)
+        dot_t(BANKS - 1)
+        n2 = nn[:, 0:1]
+        ts2(pr[:], n2, 1.0 / 5040.0, 1.0 / 120.0, ALU.mult, ALU.add)
+        ts2(pr[:], pr[:], n2, 1.0 / 6.0, ALU.mult, ALU.add)
+        ts2(pr[:], pr[:], n2, 1.0, ALU.mult, ALU.add)
+        ts1(mkr[:], n2, 1.0 / 16.0, ALU.is_lt)
+        tt(pr[:], pr[:], mkr[:], ALU.mult)
+        ts2(qsel[:], mkr[:], -0.5, 0.5, ALU.mult, ALU.add)
+        nc.vector.tensor_reduce(out=d0[:], in_=s2[:], axis=AX.X, op=ALU.add)
+        ts1(qc[:], rq[:, 1:2], 1.0e6, ALU.min)
+        tt(w1[:], d0[:], qc[:], ALU.mult)
+        ts2(tf[:], th[:], w1[:], gw[:], ALU.mult, ALU.add)
+        stt(small[:], pr[:], rq[:, 0:1], qc[:], ALU.mult, ALU.mult)
+        tt(qsel[:], qsel[:], qc[:], ALU.mult)
+        tt(smt[:], small[:], tf[:], ALU.mult)
+        stt(sh[:], er[:], eri[:], qsel[:], ALU.subtract, ALU.mult)
+        stt(fac[:], sh[:], tf[:], smt[:], ALU.mult, ALU.add)
+
+        for j in range(BANKS):
+            cols = slice(j * BANK, (j + 1) * BANK)
+            stt(o_sb[:, cols], acc[j][:], fac[:], t_sb[:, cols], ALU.mult, ALU.add)
+            nc.sync.dma_start(out=out[:, cols], in_=o_sb[:, cols])

@@ -91,9 +91,13 @@ def tile_pvfc_w_kernel(tc, x, W_words, W_scales, b, out):
                     out=planes[h][32 * q:32 * q + 16, :].bitcast(I32),
                     in_=W_scales[4 * h:4 * h + 4, 4 * q:4 * q + 4, :].bitcast(I32),
                 )
-        chunks = [(g, 0, N) for g in range(GROUPS - 1)]
-        chunks.extend([(GROUPS - 1, j * BANK, (j + 1) * BANK) for j in range(BANKS)])
-        for g, n0, n1 in chunks:
+        chunks = [(g, 0, BANKS) for g in range(GROUPS - 2)]
+        for jj in range(3):
+            chunks.extend([(g, 2 * jj, 2 * jj + 2) for g in (GROUPS - 2, GROUPS - 1)])
+        for j in (BANKS - 2, BANKS - 1):
+            chunks.extend([(g, j, j + 1) for g in (GROUPS - 2, GROUPS - 1)])
+        for g, j0, j1 in chunks:
+            n0, n1 = j0 * BANK, j1 * BANK
             nc.sync.dma_start(
                 out=w[g][:, n0:n1].bitcast(I32),
                 in_=W_words[g, :, n0:n1, :].rearrange("p n t -> p (n t)").bitcast(I32),
@@ -182,27 +186,21 @@ def tile_pvfc_w_kernel(tc, x, W_words, W_scales, b, out):
         zz = col("zz", 2)
         ez = col("ez")
         ezi = col("ezi")
-        pz = col("pz")
-        mkz = col("mkz")
-        qz = col("qz")
-        bigz = col("bigz")
+        thz = col("thz")
+        cz = col("cz")
+        hz = col("hz")
         sc = col("sc")
         g2 = col("g2")
         gw = col("gw")
         nc.scalar.activation(out=t_sb[:], in_=b_bc[:], func=ACT.Square, accum_out=bb[:])
         ts2(bz2[:], bb[:, 0:1].to_broadcast([P, 2]), 1e-15, 400.0, ALU.max, ALU.min)
         nc.gpsimd.tensor_tensor(out=zz[:], in0=bz2[:], in1=pw3[:, 1:3], op=ALU.pow)
-        nc.scalar.activation(out=ez[:], in_=zz[:, 0:1], func=ACT.Exp)
+        nc.scalar.activation(out=thz[:], in_=zz[:, 0:1], func=ACT.Tanh, scale=0.5)
         nc.scalar.activation(out=ezi[:], in_=zz[:, 0:1], func=ACT.Exp, scale=-1.0)
-        bz = bz2[:, 0:1]
-        ts2(pz[:], bz, 1.0 / 5040.0, 1.0 / 120.0, ALU.mult, ALU.add)
-        ts2(pz[:], pz[:], bz, 1.0 / 6.0, ALU.mult, ALU.add)
-        ts2(pz[:], pz[:], bz, 1.0, ALU.mult, ALU.add)
-        ts1(mkz[:], bz, 1.0 / 16.0, ALU.is_lt)
-        ts2(qz[:], mkz[:], -0.5, 0.5, ALU.mult, ALU.add)
-        tt(qz[:], qz[:], zz[:, 1:2], ALU.mult)
-        stt(bigz[:], ez[:], ezi[:], qz[:], ALU.subtract, ALU.mult)
-        stt(sc[:], pz[:], mkz[:], bigz[:], ALU.mult, ALU.add)
+        nc.scalar.activation(out=ez[:], in_=zz[:, 0:1], func=ACT.Exp)
+        tt(hz[:], thz[:], zz[:, 1:2], ALU.mult)
+        stt(cz[:], ez[:], 2.0, ezi[:], ALU.add, ALU.add)
+        stt(sc[:], cz[:], 0.5, hz[:], ALU.mult, ALU.mult)
         tt(g2[:], sc[:], sc[:], ALU.mult)
         ts2(g2[:], g2[:], bb[:], 1.0, ALU.mult, ALU.add)
         nc.gpsimd.tensor_tensor(out=gw[:], in0=g2[:], in1=pw3[:, 0:1], op=ALU.pow)
@@ -222,13 +220,6 @@ def tile_pvfc_w_kernel(tc, x, W_words, W_scales, b, out):
                 stop=(g == GROUPS - 1),
             )
 
-        for j in range(BANKS):
-            acc[j] = psum.tile([P, BANK], F32, name="acc%d" % j, tag="bk%d" % j)
-            mx_pass(0, j)
-        for g in range(1, GROUPS - 1):
-            for j in range(BANKS):
-                mx_pass(g, j)
-
         s1 = col("s1", BANKS)
         s2 = col("s2", BANKS)
 
@@ -238,51 +229,47 @@ def tile_pvfc_w_kernel(tc, x, W_words, W_scales, b, out):
                 op0=ALU.mult, op1=ALU.mult, accum_out=s2[:, j:j + 1],
             )
 
-        for j in range(BANKS):
-            mx_pass(GROUPS - 1, j)
-            nc.scalar.activation(out=junk_s[:], in_=acc[j][:], func=ACT.Square, accum_out=s1[:, j:j + 1])
-            if j < BANKS - 1:
-                dot_t(j)
+        last = BANKS - 1
+        for g, j0, j1 in chunks:
+            for j in range(j0, j1):
+                if g == 0:
+                    acc[j] = psum.tile([P, BANK], F32, name="acc%d" % j, tag="bk%d" % j)
+                mx_pass(g, j)
+            if g == GROUPS - 1:
+                for j in range(j0, j1):
+                    nc.scalar.activation(out=junk_s[:], in_=acc[j][:], func=ACT.Square, accum_out=s1[:, j:j + 1])
+                    if j < last:
+                        dot_t(j)
 
+        n2a = col("n2a")
+        d0a = col("d0a")
         nn = col("nn", 2)
         rq = col("rq", 2)
-        pr = col("pr")
-        mkr = col("mkr")
-        qsel = col("qsel")
         qc = col("qc")
         d0 = col("d0")
-        w1 = col("w1")
-        small = col("small")
         th = col("th")
         er = col("er")
         eri = col("eri")
+        hq = col("hq")
         tf = col("tf")
-        smt = col("smt")
-        sh = col("sh")
+        hf = col("hf")
+        c2 = col("c2")
         fac = col("fac")
-        nc.vector.tensor_reduce(out=nn[:], in_=s1[:].unsqueeze(1).to_broadcast([P, 2, BANKS]), axis=AX.X, op=ALU.add)
-        tt(nn[:], nn[:], hi2[:], ALU.min)
+        nc.vector.tensor_reduce(out=n2a[:], in_=s1[:, 0:last], axis=AX.X, op=ALU.add)
+        nc.vector.tensor_reduce(out=d0a[:], in_=s2[:, 0:last], axis=AX.X, op=ALU.add)
+        stt(nn[:], s1[:, last:last + 1].to_broadcast([P, 2]), n2a[:], hi2[:], ALU.add, ALU.min)
         nc.gpsimd.tensor_tensor(out=rq[:], in0=nn[:], in1=pw3[:, 1:3], op=ALU.pow)
         nc.scalar.activation(out=th[:], in_=rq[:, 0:1], func=ACT.Tanh, scale=0.5)
         nc.scalar.activation(out=eri[:], in_=rq[:, 0:1], func=ACT.Exp, scale=-1.0)
         nc.scalar.activation(out=er[:], in_=rq[:, 0:1], func=ACT.Exp)
-        dot_t(BANKS - 1)
-        n2 = nn[:, 0:1]
-        ts2(pr[:], n2, 1.0 / 5040.0, 1.0 / 120.0, ALU.mult, ALU.add)
-        ts2(pr[:], pr[:], n2, 1.0 / 6.0, ALU.mult, ALU.add)
-        ts2(pr[:], pr[:], n2, 1.0, ALU.mult, ALU.add)
-        ts1(mkr[:], n2, 1.0 / 16.0, ALU.is_lt)
-        tt(pr[:], pr[:], mkr[:], ALU.mult)
-        ts2(qsel[:], mkr[:], -0.5, 0.5, ALU.mult, ALU.add)
-        nc.vector.tensor_reduce(out=d0[:], in_=s2[:], axis=AX.X, op=ALU.add)
+        dot_t(last)
+        tt(d0[:], d0a[:], s2[:, last:last + 1], ALU.add)
         ts1(qc[:], rq[:, 1:2], 1.0e6, ALU.min)
-        tt(w1[:], d0[:], qc[:], ALU.mult)
-        ts2(tf[:], th[:], w1[:], gw[:], ALU.mult, ALU.add)
-        stt(small[:], pr[:], rq[:, 0:1], qc[:], ALU.mult, ALU.mult)
-        tt(qsel[:], qsel[:], qc[:], ALU.mult)
-        tt(smt[:], small[:], tf[:], ALU.mult)
-        stt(sh[:], er[:], eri[:], qsel[:], ALU.subtract, ALU.mult)
-        stt(fac[:], sh[:], tf[:], smt[:], ALU.mult, ALU.add)
+        tt(hq[:], th[:], qc[:], ALU.mult)
+        ts2(tf[:], hq[:], d0[:], gw[:], ALU.mult, ALU.add)
+        stt(hf[:], hq[:], 0.5, tf[:], ALU.mult, ALU.mult)
+        stt(c2[:], er[:], 2.0, eri[:], ALU.add, ALU.add)
+        tt(fac[:], c2[:], hf[:], ALU.mult)
 
         for j in range(BANKS):
             cols = slice(j * BANK, (j + 1) * BANK)

@@ -87,10 +87,12 @@ def tile_pvfc_w_kernel(tc, x, W_words, W_scales, b, out):
         nc.scalar.dma_start(out=brow[0:1, :], in_=b.unsqueeze(0))
         for h in range(2):
             for q in range(4):
-                nc.sync.dma_start(
-                    out=planes[h][32 * q:32 * q + 16, :].bitcast(I32),
-                    in_=W_scales[4 * h:4 * h + 4, 4 * q:4 * q + 4, :].bitcast(I32),
-                )
+                for c in range(2):
+                    cols = slice(c * (N // 2), (c + 1) * (N // 2))
+                    nc.sync.dma_start(
+                        out=planes[h][32 * q:32 * q + 16, cols].bitcast(I32),
+                        in_=W_scales[4 * h:4 * h + 4, 4 * q:4 * q + 4, cols].bitcast(I32),
+                    )
         chunks = [(g, 0, BANKS) for g in range(GROUPS - 2)]
         for jj in range(3):
             chunks.extend([(g, 2 * jj, 2 * jj + 2) for g in (GROUPS - 2, GROUPS - 1)])

@@ -87,12 +87,10 @@ def tile_pvfc_w_kernel(tc, x, W_words, W_scales, b, out):
         nc.scalar.dma_start(out=brow[0:1, :], in_=b.unsqueeze(0))
         for h in range(2):
             for q in range(4):
-                for c in range(2):
-                    cols = slice(c * (N // 2), (c + 1) * (N // 2))
-                    nc.sync.dma_start(
-                        out=planes[h][32 * q:32 * q + 16, cols].bitcast(I32),
-                        in_=W_scales[4 * h:4 * h + 4, 4 * q:4 * q + 4, cols].bitcast(I32),
-                    )
+                nc.sync.dma_start(
+                    out=planes[h][32 * q:32 * q + 16, :].bitcast(I32),
+                    in_=W_scales[4 * h:4 * h + 4, 4 * q:4 * q + 4, :].bitcast(I32),
+                )
         chunks = [(g, 0, BANKS) for g in range(GROUPS - 2)]
         for jj in range(3):
             chunks.extend([(g, 2 * jj, 2 * jj + 2) for g in (GROUPS - 2, GROUPS - 1)])
@@ -247,14 +245,14 @@ def tile_pvfc_w_kernel(tc, x, W_words, W_scales, b, out):
         d0a = col("d0a")
         nn = col("nn", 2)
         rq = col("rq", 2)
-        qc = col("qc")
+        qd = col("qd")
+        qh = col("qh")
         d0 = col("d0")
         th = col("th")
         er = col("er")
         eri = col("eri")
-        hq = col("hq")
         tf = col("tf")
-        hf = col("hf")
+        hh = col("hh")
         c2 = col("c2")
         fac = col("fac")
         nc.vector.tensor_reduce(out=n2a[:], in_=s1[:, 0:last], axis=AX.X, op=ALU.add)
@@ -266,12 +264,12 @@ def tile_pvfc_w_kernel(tc, x, W_words, W_scales, b, out):
         nc.scalar.activation(out=er[:], in_=rq[:, 0:1], func=ACT.Exp)
         dot_t(last)
         tt(d0[:], d0a[:], s2[:, last:last + 1], ALU.add)
-        ts1(qc[:], rq[:, 1:2], 1.0e6, ALU.min)
-        tt(hq[:], th[:], qc[:], ALU.mult)
-        ts2(tf[:], hq[:], d0[:], gw[:], ALU.mult, ALU.add)
-        stt(hf[:], hq[:], 0.5, tf[:], ALU.mult, ALU.mult)
+        ts2(qd[:], rq[:, 1:2], 1.0e6, d0[:], ALU.min, ALU.mult)
+        ts2(qh[:], rq[:, 1:2], 1.0e6, 0.5, ALU.min, ALU.mult)
+        ts2(tf[:], th[:], qd[:], gw[:], ALU.mult, ALU.add)
+        tt(hh[:], th[:], qh[:], ALU.mult)
         stt(c2[:], er[:], 2.0, eri[:], ALU.add, ALU.add)
-        tt(fac[:], c2[:], hf[:], ALU.mult)
+        stt(fac[:], c2[:], hh[:], tf[:], ALU.mult, ALU.mult)
 
         for j in range(BANKS):
             cols = slice(j * BANK, (j + 1) * BANK)

@@ -91,11 +91,12 @@ def tile_pvfc_w_kernel(tc, x, W_words, W_scales, b, out):
                     out=planes[h][32 * q:32 * q + 16, :].bitcast(I32),
                     in_=W_scales[4 * h:4 * h + 4, 4 * q:4 * q + 4, :].bitcast(I32),
                 )
-        chunks = [(g, 0, BANKS) for g in range(GROUPS - 2)]
+        stair = (GROUPS - 3, GROUPS - 2, GROUPS - 1)
+        chunks = [(g, 0, BANKS) for g in range(GROUPS - 3)]
         for jj in range(3):
-            chunks.extend([(g, 2 * jj, 2 * jj + 2) for g in (GROUPS - 2, GROUPS - 1)])
+            chunks.extend([(g, 2 * jj, 2 * jj + 2) for g in stair])
         for j in (BANKS - 2, BANKS - 1):
-            chunks.extend([(g, j, j + 1) for g in (GROUPS - 2, GROUPS - 1)])
+            chunks.extend([(g, j, j + 1) for g in stair])
         for g, j0, j1 in chunks:
             n0, n1 = j0 * BANK, j1 * BANK
             nc.sync.dma_start(

@@ -1,3 +1,4 @@
+import math
 from contextlib import ExitStack
 
 import concourse.masks as masks
@@ -64,7 +65,7 @@ def tile_pvfc_w_kernel(tc, x, W_words, W_scales, b, out):
         coef_bc = big.tile([P, P], F32, name="coef_bc")
 
         pw3 = col("pw3", 3)
-        hi2 = col("hi2", 2)
+        cv3 = col("cv3", 3)
         one1 = col("one1")
         scr1 = col("scr1")
 
@@ -76,8 +77,9 @@ def tile_pvfc_w_kernel(tc, x, W_words, W_scales, b, out):
         nc.vector.memset(brow[:].bitcast(I32), 0)
         nc.vector.memset(pw3[:, 0:2], 0.5)
         nc.vector.memset(pw3[:, 2:3], -0.5)
-        nc.vector.memset(hi2[:, 0:1], 400.0)
-        nc.vector.memset(hi2[:, 1:2], 3.0e38)
+        nc.vector.memset(cv3[:, 0:1], 1.0)
+        nc.vector.memset(cv3[:, 1:2], 0.5)
+        nc.vector.memset(cv3[:, 2:3], -1.0)
         nc.vector.memset(ones_bf[:], 1.0)
         nc.vector.memset(ones_f[:], 1.0)
 
@@ -205,6 +207,8 @@ def tile_pvfc_w_kernel(tc, x, W_words, W_scales, b, out):
         tt(g2[:], sc[:], sc[:], ALU.mult)
         ts2(g2[:], g2[:], bb[:], 1.0, ALU.mult, ALU.add)
         nc.gpsimd.tensor_tensor(out=gw[:], in0=g2[:], in1=pw3[:, 0:1], op=ALU.pow)
+        gwh = col("gwh")
+        ts1(gwh[:], gw[:], 0.5, ALU.mult)
         nc.scalar.activation(out=t_sb[:], in_=b_bc[:], func=ACT.Copy, scale=sc[:])
 
         acc = [None] * BANKS
@@ -231,6 +235,11 @@ def tile_pvfc_w_kernel(tc, x, W_words, W_scales, b, out):
             )
 
         last = BANKS - 1
+        n2a = col("n2a")
+        na3 = col("na3", 3)
+        nb3 = col("nb3", 3)
+        d0a = col("d0a")
+        d0x = col("d0x")
         for g, j0, j1 in chunks:
             for j in range(j0, j1):
                 if g == 0:
@@ -239,38 +248,40 @@ def tile_pvfc_w_kernel(tc, x, W_words, W_scales, b, out):
             if g == GROUPS - 1:
                 for j in range(j0, j1):
                     nc.scalar.activation(out=junk_s[:], in_=acc[j][:], func=ACT.Square, accum_out=s1[:, j:j + 1])
+                    if j == last - 1:
+                        stt(nb3[:], cv3[:], s1[:, j:j + 1], na3[:], ALU.mult, ALU.add)
                     if j < last:
                         dot_t(j)
+                    if j == last - 2:
+                        nc.vector.tensor_reduce(out=n2a[:], in_=s1[:, 0:last - 1], axis=AX.X, op=ALU.add)
+                        stt(na3[:], n2a[:, 0:1].to_broadcast([P, 3]), 1e-12, cv3[:], ALU.max, ALU.mult)
+                        nc.vector.tensor_reduce(out=d0a[:], in_=s2[:, 0:last - 1], axis=AX.X, op=ALU.add)
+                    if j == last - 1:
+                        ts2(d0x[:], s2[:, j:j + 1], d0a[:], 0.5, ALU.add, ALU.mult)
 
-        n2a = col("n2a")
-        d0a = col("d0a")
-        nn = col("nn", 2)
-        rq = col("rq", 2)
-        qd = col("qd")
-        qh = col("qh")
-        d0 = col("d0")
+        nn3 = col("nn3", 3)
+        q = col("q")
+        d0h = col("d0h")
         th = col("th")
         er = col("er")
         eri = col("eri")
-        tf = col("tf")
-        hh = col("hh")
+        eri2 = col("eri2")
+        yq = col("yq")
+        wq = col("wq")
         c2 = col("c2")
         fac = col("fac")
-        nc.vector.tensor_reduce(out=n2a[:], in_=s1[:, 0:last], axis=AX.X, op=ALU.add)
-        nc.vector.tensor_reduce(out=d0a[:], in_=s2[:, 0:last], axis=AX.X, op=ALU.add)
-        stt(nn[:], s1[:, last:last + 1].to_broadcast([P, 2]), n2a[:], hi2[:], ALU.add, ALU.min)
-        nc.gpsimd.tensor_tensor(out=rq[:], in0=nn[:], in1=pw3[:, 1:3], op=ALU.pow)
-        nc.scalar.activation(out=th[:], in_=rq[:, 0:1], func=ACT.Tanh, scale=0.5)
-        nc.scalar.activation(out=eri[:], in_=rq[:, 0:1], func=ACT.Exp, scale=-1.0)
-        nc.scalar.activation(out=er[:], in_=rq[:, 0:1], func=ACT.Exp)
+        stt(nn3[:], cv3[:], s1[:, last:last + 1], nb3[:], ALU.mult, ALU.add)
+        nc.gpsimd.tensor_tensor(out=q[:], in0=nn3[:, 0:1], in1=pw3[:, 2:3], op=ALU.pow)
+        nc.scalar.activation(out=eri[:], in_=nn3[:, 2:3], func=ACT.Exp, scale=q[:])
+        nc.scalar.activation(out=th[:], in_=nn3[:, 1:2], func=ACT.Tanh, scale=q[:])
+        nc.scalar.activation(out=er[:], in_=nn3[:, 0:1], func=ACT.Exp, scale=q[:])
         dot_t(last)
-        tt(d0[:], d0a[:], s2[:, last:last + 1], ALU.add)
-        ts2(qd[:], rq[:, 1:2], 1.0e6, d0[:], ALU.min, ALU.mult)
-        ts2(qh[:], rq[:, 1:2], 1.0e6, 0.5, ALU.min, ALU.mult)
-        ts2(tf[:], th[:], qd[:], gw[:], ALU.mult, ALU.add)
-        tt(hh[:], th[:], qh[:], ALU.mult)
-        stt(c2[:], er[:], 2.0, eri[:], ALU.add, ALU.add)
-        stt(fac[:], c2[:], hh[:], tf[:], ALU.mult, ALU.mult)
+        ts2(d0h[:], s2[:, last:last + 1], 0.5, d0x[:], ALU.mult, ALU.add)
+        ts1(eri2[:], eri[:], 2.0, ALU.add)
+        tt(yq[:], th[:], q[:], ALU.mult)
+        ts2(wq[:], yq[:], d0h[:], gwh[:], ALU.mult, ALU.add)
+        stt(c2[:], er[:], math.e ** 20.0, eri2[:], ALU.min, ALU.add)
+        stt(fac[:], c2[:], yq[:], wq[:], ALU.mult, ALU.mult)
 
         for j in range(BANKS):
             cols = slice(j * BANK, (j + 1) * BANK)

@@ -84,8 +84,7 @@ def tile_pvfc_w_kernel(tc, x, W_words, W_scales, b, out):
         nc.vector.memset(ones_f[:], 1.0)
 
         half = K // 2
-        for h in range(2):
-            nc.sync.dma_start(out=x_sb[:, h * half:(h + 1) * half], in_=x[:, h * half:(h + 1) * half])
+        nc.sync.dma_start(out=x_sb[:], in_=x[:, :])
         nc.scalar.dma_start(out=brow[0:1, :], in_=b.unsqueeze(0))
         for h in range(2):
             for q in range(4):
@@ -93,12 +92,11 @@ def tile_pvfc_w_kernel(tc, x, W_words, W_scales, b, out):
                     out=planes[h][32 * q:32 * q + 16, :].bitcast(I32),
                     in_=W_scales[4 * h:4 * h + 4, 4 * q:4 * q + 4, :].bitcast(I32),
                 )
-        stair = (GROUPS - 3, GROUPS - 2, GROUPS - 1)
-        chunks = [(g, 0, BANKS) for g in range(GROUPS - 3)]
-        for jj in range(3):
-            chunks.extend([(g, 2 * jj, 2 * jj + 2) for g in stair])
-        for j in (BANKS - 2, BANKS - 1):
-            chunks.extend([(g, j, j + 1) for g in stair])
+        chunks = [(g, 0, BANKS) for g in range(GROUPS - 4)]
+        chunks.extend([(g, 0, BANKS - 1) for g in (GROUPS - 4, GROUPS - 3)])
+        for j0, j1 in ((0, 2), (2, 4), (4, 6), (6, 7)):
+            chunks.extend([(g, j0, j1) for g in (GROUPS - 2, GROUPS - 1)])
+        chunks.extend([(g, BANKS - 1, BANKS) for g in range(GROUPS - 4, GROUPS)])
         for g, j0, j1 in chunks:
             n0, n1 = j0 * BANK, j1 * BANK
             nc.sync.dma_start(

@@ -56,8 +56,8 @@ def tile_pvfc_w_kernel(tc, x, W_words, W_scales, b, out):
         v_scales = big.tile([P, GROUPS * P], U8, name="v_scales", align_bytes=64)
         planes = [big.tile([P, N], U8, name="planes%d" % h, align_bytes=64) for h in range(2)]
         w = [big.tile([P, N], U32, name="w%d" % g, align_bytes=64) for g in range(GROUPS)]
-        junk_s = big.tile([P, BANK], F32, name="junk_s")
-        junk_v = big.tile([P, BANK], F32, name="junk_v")
+        squares = [big.tile([P, BANK], F32, name="squares%d" % i) for i in range(4)]
+        products = [big.tile([P, BANK], F32, name="products%d" % i) for i in range(4)]
         ident = big.tile([P, P], F32, name="ident")
         ones_bf = big.tile([P, P], BF16, name="ones_bf")
         ones_f = big.tile([P, P], F32, name="ones_f")
@@ -228,7 +228,7 @@ def tile_pvfc_w_kernel(tc, x, W_words, W_scales, b, out):
 
         def dot_t(j):
             nc.vector.scalar_tensor_tensor(
-                out=junk_v[:], in0=acc[j][:], scalar=1.0, in1=t_sb[:, j * BANK:(j + 1) * BANK],
+                out=products[j % 4][:], in0=acc[j][:], scalar=1.0, in1=t_sb[:, j * BANK:(j + 1) * BANK],
                 op0=ALU.mult, op1=ALU.mult, accum_out=s2[:, j:j + 1],
             )
 
@@ -245,7 +245,7 @@ def tile_pvfc_w_kernel(tc, x, W_words, W_scales, b, out):
                 mx_pass(g, j)
             if g == GROUPS - 1:
                 for j in range(j0, j1):
-                    nc.scalar.activation(out=junk_s[:], in_=acc[j][:], func=ACT.Square, accum_out=s1[:, j:j + 1])
+                    nc.scalar.activation(out=squares[j % 4][:], in_=acc[j][:], func=ACT.Square, accum_out=s1[:, j:j + 1])
                     if j == last - 1:
                         stt(nb3[:], cv3[:], s1[:, j:j + 1], na3[:], ALU.mult, ALU.add)
                     if j < last:

@@ -92,11 +92,9 @@ def tile_pvfc_w_kernel(tc, x, W_words, W_scales, b, out):
                     out=planes[h][32 * q:32 * q + 16, :].bitcast(I32),
                     in_=W_scales[4 * h:4 * h + 4, 4 * q:4 * q + 4, :].bitcast(I32),
                 )
-        chunks = [(g, 0, BANKS) for g in range(GROUPS - 4)]
-        chunks.extend([(g, 0, BANKS - 1) for g in (GROUPS - 4, GROUPS - 3)])
-        for j0, j1 in ((0, 2), (2, 4), (4, 6), (6, 7)):
+        chunks = [(g, 0, BANKS) for g in range(GROUPS - 2)]
+        for j0, j1 in ((0, 2), (2, 4), (4, 6), (6, 7), (7, 8)):
             chunks.extend([(g, j0, j1) for g in (GROUPS - 2, GROUPS - 1)])
-        chunks.extend([(g, BANKS - 1, BANKS) for g in range(GROUPS - 4, GROUPS)])
         for g, j0, j1 in chunks:
             n0, n1 = j0 * BANK, j1 * BANK
             nc.sync.dma_start(
@@ -205,8 +203,6 @@ def tile_pvfc_w_kernel(tc, x, W_words, W_scales, b, out):
         tt(g2[:], sc[:], sc[:], ALU.mult)
         ts2(g2[:], g2[:], bb[:], 1.0, ALU.mult, ALU.add)
         nc.gpsimd.tensor_tensor(out=gw[:], in0=g2[:], in1=pw3[:, 0:1], op=ALU.pow)
-        gwh = col("gwh")
-        ts1(gwh[:], gw[:], 0.5, ALU.mult)
         nc.scalar.activation(out=t_sb[:], in_=b_bc[:], func=ACT.Copy, scale=sc[:])
 
         acc = [None] * BANKS
@@ -234,10 +230,9 @@ def tile_pvfc_w_kernel(tc, x, W_words, W_scales, b, out):
 
         last = BANKS - 1
         n2a = col("n2a")
-        na3 = col("na3", 3)
+        n2b = col("n2b")
         nb3 = col("nb3", 3)
         d0a = col("d0a")
-        d0x = col("d0x")
         for g, j0, j1 in chunks:
             for j in range(j0, j1):
                 if g == 0:
@@ -247,24 +242,28 @@ def tile_pvfc_w_kernel(tc, x, W_words, W_scales, b, out):
                 for j in range(j0, j1):
                     nc.scalar.activation(out=squares[j % 4][:], in_=acc[j][:], func=ACT.Square, accum_out=s1[:, j:j + 1])
                     if j == last - 1:
-                        stt(nb3[:], cv3[:], s1[:, j:j + 1], na3[:], ALU.mult, ALU.add)
-                    if j < last:
+                        stt(nb3[:], s1[:, j:j + 1].to_broadcast([P, 3]), n2b[:], cv3[:], ALU.add, ALU.mult)
+                        tt(products[j % 4][:], acc[j][:], t_sb[:, j * BANK:(j + 1) * BANK], ALU.mult)
+                    elif j < last:
                         dot_t(j)
-                    if j == last - 2:
-                        nc.vector.tensor_reduce(out=n2a[:], in_=s1[:, 0:last - 1], axis=AX.X, op=ALU.add)
-                        stt(na3[:], n2a[:, 0:1].to_broadcast([P, 3]), 1e-12, cv3[:], ALU.max, ALU.mult)
-                        nc.vector.tensor_reduce(out=d0a[:], in_=s2[:, 0:last - 1], axis=AX.X, op=ALU.add)
-                    if j == last - 1:
-                        ts2(d0x[:], s2[:, j:j + 1], d0a[:], 0.5, ALU.add, ALU.mult)
+                    if j == 3:
+                        nc.vector.tensor_reduce(out=n2a[:], in_=s1[:, 0:4], axis=AX.X, op=ALU.add)
+                        ts1(n2a[:], n2a[:], 1e-12, ALU.max)
+                    if j == 5:
+                        ts2(n2b[:], n2a[:], s1[:, 4:5], s1[:, 5:6], ALU.add, ALU.add)
+                    if j == last:
+                        nc.scalar.activation(out=squares[(j + 1) % 4][:], in_=products[(j - 1) % 4][:], func=ACT.Copy,
+                                             accum_out=s2[:, j - 1:j])
 
         nn3 = col("nn3", 3)
         q = col("q")
-        d0h = col("d0h")
+        dot = col("dot")
         th = col("th")
         er = col("er")
         eri = col("eri")
         eri2 = col("eri2")
         yq = col("yq")
+        yqh = col("yqh")
         wq = col("wq")
         c2 = col("c2")
         fac = col("fac")
@@ -273,13 +272,15 @@ def tile_pvfc_w_kernel(tc, x, W_words, W_scales, b, out):
         nc.scalar.activation(out=eri[:], in_=nn3[:, 2:3], func=ACT.Exp, scale=q[:])
         nc.scalar.activation(out=th[:], in_=nn3[:, 1:2], func=ACT.Tanh, scale=q[:])
         nc.scalar.activation(out=er[:], in_=nn3[:, 0:1], func=ACT.Exp, scale=q[:])
+        nc.vector.tensor_reduce(out=d0a[:], in_=s2[:, 0:last - 1], axis=AX.X, op=ALU.add)
         dot_t(last)
-        ts2(d0h[:], s2[:, last:last + 1], 0.5, d0x[:], ALU.mult, ALU.add)
+        ts2(dot[:], s2[:, last:last + 1], s2[:, last - 1:last], d0a[:], ALU.add, ALU.add)
         ts1(eri2[:], eri[:], 2.0, ALU.add)
         tt(yq[:], th[:], q[:], ALU.mult)
-        ts2(wq[:], yq[:], d0h[:], gwh[:], ALU.mult, ALU.add)
+        stt(yqh[:], th[:], 0.5, q[:], ALU.mult, ALU.mult)
+        ts2(wq[:], yq[:], dot[:], gw[:], ALU.mult, ALU.add)
         stt(c2[:], er[:], math.e ** 20.0, eri2[:], ALU.min, ALU.add)
-        stt(fac[:], c2[:], yq[:], wq[:], ALU.mult, ALU.mult)
+        stt(fac[:], c2[:], yqh[:], wq[:], ALU.mult, ALU.mult)
 
         for j in range(BANKS):
             cols = slice(j * BANK, (j + 1) * BANK)

import math
from contextlib import ExitStack

import concourse.masks as masks
import concourse.mybir as mybir

F32 = mybir.dt.float32
BF16 = mybir.dt.bfloat16
I32 = mybir.dt.int32
U32 = mybir.dt.uint32
U8 = mybir.dt.uint8
FP8X4 = mybir.dt.float8_e4m3fn_x4
ALU = mybir.AluOpType
ACT = mybir.ActivationFunctionType
AX = mybir.AxisListType

P = 128
M, K, N = 128, 4096, 4096
K_PASS = 512
GROUPS = K // K_PASS
BANK = 512
BANKS = N // BANK
FLOPS = 2 * M * K * N


def tile_pvfc_w_kernel(tc, x, W_words, W_scales, b, out):
    nc = tc.nc
    with ExitStack() as ctx:
        ctx.enter_context(tc.manual_schedule())
        big = ctx.enter_context(tc.tile_pool(name="big", bufs=1))
        sm = ctx.enter_context(tc.tile_pool(name="sm", bufs=1))
        psum = ctx.enter_context(tc.psum_pool(name="psum", bufs=1))

        def col(name, width=1):
            return sm.tile([P, width], F32, name=name)

        def ts2(o, i, s1, s2, op0, op1):
            nc.vector.tensor_scalar(out=o, in0=i, scalar1=s1, scalar2=s2, op0=op0, op1=op1)

        def ts1(o, i, s1, op0):
            nc.vector.tensor_scalar(out=o, in0=i, scalar1=s1, scalar2=None, op0=op0)

        def stt(o, i0, s, i1, op0, op1):
            nc.vector.scalar_tensor_tensor(out=o, in0=i0, scalar=s, in1=i1, op0=op0, op1=op1)

        def tt(o, i0, i1, op):
            nc.vector.tensor_tensor(out=o, in0=i0, in1=i1, op=op)

        x_sb = big.tile([P, K], BF16, name="x_sb")
        brow = big.tile([P, N], BF16, name="brow")
        b_bc = big.tile([P, N], BF16, name="b_bc")
        t_sb = big.tile([P, N], F32, name="t_sb")
        o_sb = big.tile([P, N], F32, name="o_sb")
        grouped = big.tile([P, GROUPS, K_PASS], BF16, name="grouped", align_bytes=64)
        v_codes = big.tile([P, GROUPS * P], U32, name="v_codes", align_bytes=64)
        v_scales = big.tile([P, GROUPS * P], U8, name="v_scales", align_bytes=64)
        planes = [big.tile([P, N], U8, name="planes%d" % h, align_bytes=64) for h in range(2)]
        w = [big.tile([P, N], U32, name="w%d" % g, align_bytes=64) for g in range(GROUPS)]
        squares = [big.tile([P, BANK], F32, name="squares%d" % i) for i in range(4)]
        products = [big.tile([P, BANK], F32, name="products%d" % i) for i in range(4)]
        ident = big.tile([P, P], F32, name="ident")
        ones_bf = big.tile([P, P], BF16, name="ones_bf")
        ones_f = big.tile([P, P], F32, name="ones_f")
        rep = big.tile([P, P], F32, name="rep")
        coef_bc = big.tile([P, P], F32, name="coef_bc")

        pw3 = col("pw3", 3)
        cv3 = col("cv3", 3)
        one1 = col("one1")
        scr1 = col("scr1")

        nc.vector.memset(one1[:], 1.0)
        nc.scalar.activation(out=scr1[:], in_=one1[:], func=ACT.Ln)
        masks.make_identity(nc, ident[:])
        for h in range(2):
            nc.vector.memset(planes[h][:].bitcast(I32), 0)
        nc.vector.memset(brow[:].bitcast(I32), 0)
        nc.vector.memset(pw3[:, 0:2], 0.5)
        nc.vector.memset(pw3[:, 2:3], -0.5)
        nc.vector.memset(cv3[:, 0:1], 1.0)
        nc.vector.memset(cv3[:, 1:2], 0.5)
        nc.vector.memset(cv3[:, 2:3], -1.0)
        nc.vector.memset(ones_bf[:], 1.0)
        nc.vector.memset(ones_f[:], 1.0)

        half = K // 2
        nc.sync.dma_start(out=x_sb[:], in_=x[:, :])
        nc.scalar.dma_start(out=brow[0:1, :], in_=b.unsqueeze(0))
        for h in range(2):
            for q in range(4):
                nc.sync.dma_start(
                    out=planes[h][32 * q:32 * q + 16, :].bitcast(I32),
                    in_=W_scales[4 * h:4 * h + 4, 4 * q:4 * q + 4, :].bitcast(I32),
                )
        chunks = [(g, 0, BANKS) for g in range(GROUPS - 2)]
        for j0, j1 in ((0, 2), (2, 4), (4, 6), (6, 7), (7, 8)):
            chunks.extend([(g, j0, j1) for g in (GROUPS - 2, GROUPS - 1)])
        for g, j0, j1 in chunks:
            n0, n1 = j0 * BANK, j1 * BANK
            nc.sync.dma_start(
                out=w[g][:, n0:n1].bitcast(I32),
                in_=W_words[g, :, n0:n1, :].rearrange("p n t -> p (n t)").bitcast(I32),
            )

        ssv = col("ssv")
        sss = col("sss")
        nc.vector.scalar_tensor_tensor(
            out=o_sb[:, 0:half], in0=x_sb[:, 0:half], scalar=1.0, in1=x_sb[:, 0:half],
            op0=ALU.mult, op1=ALU.mult, accum_out=ssv[:],
        )
        nc.scalar.activation(out=o_sb[:, half:K], in_=x_sb[:, half:K], func=ACT.Square, accum_out=sss[:])

        xw = x_sb[:].bitcast(F32)
        xt = []
        for i in range(4):
            xt_i = psum.tile([P, 4, P], F32, name="xt%d" % i, tag="bk%d" % (4 + i))
            xt.append(xt_i)
            for gg in range(2):
                for u in range(2):
                    g = 2 * i + gg
                    nc.tensor.transpose(xt_i[:, 2 * gg + u, :], xw[:, 256 * g + u:256 * (g + 1):2], ident[:])

        for i in range(4):
            b_ps = psum.tile([P, 2 * BANK], BF16, name="b_ps%d" % i, tag="bk%d" % i)
            for c in range(2):
                n0 = (2 * i + c) * BANK
                nc.tensor.matmul(b_ps[:, c * BANK:(c + 1) * BANK], lhsT=ones_bf[:], rhs=brow[:, n0:n0 + BANK],
                                 start=True, stop=True)
            nc.scalar.copy(out=b_bc[:, 2 * i * BANK:(2 * i + 2) * BANK], in_=b_ps[:])
            if i == 0:
                ss3 = col("ss3", 3)
                sq3 = col("sq3", 3)
                lnv = col("lnv")
                pa = col("pa")
                mkx = col("mkx")
                dx = col("dx")
                lsel = col("lsel")
                coef = col("coef")
                tt(ss3[:, 0:1], ssv[:], sss[:], ALU.add)
                ts1(ss3[:, 1:2], ss3[:, 0:1], 1.0, ALU.add)
                ts1(ss3[:, 2:3], ss3[:, 0:1], 1e-12, ALU.max)
                nc.gpsimd.tensor_tensor(out=sq3[:], in0=ss3[:], in1=pw3[:], op=ALU.pow)
                nc.scalar.activation(out=lnv[:], in_=sq3[:, 0:1], func=ACT.Ln, bias=sq3[:, 1:2], scale=1.0)
                ss = ss3[:, 0:1]
                ts2(pa[:], ss, 35.0 / 1152.0, -5.0 / 112.0, ALU.mult, ALU.add)
                ts2(pa[:], pa[:], ss, 3.0 / 40.0, ALU.mult, ALU.add)
                ts2(pa[:], pa[:], ss, -1.0 / 6.0, ALU.mult, ALU.add)
                ts2(pa[:], pa[:], ss, 1.0, ALU.mult, ALU.add)
                ts1(mkx[:], ss, 1.0 / 64.0, ALU.is_lt)
                stt(dx[:], pa[:], sq3[:, 0:1], lnv[:], ALU.mult, ALU.subtract)
                stt(lsel[:], dx[:], mkx[:], lnv[:], ALU.mult, ALU.add)
                tt(coef[:], lsel[:], sq3[:, 2:3], ALU.mult)
                ts1(rep[:], ones_f[:], coef[:], ALU.mult)

        ct = psum.tile([P, P], F32, name="ct", tag="bk0")
        nc.tensor.transpose(ct[:], rep[:], ident[:])
        nc.vector.tensor_copy(out=coef_bc[:], in_=ct[:])

        def scale_group(g):
            src = xt[g // 2][:, 2 * (g % 2):2 * (g % 2) + 2, :].bitcast(BF16)
            tt(
                grouped[:, g, :].rearrange("p (m u e) -> p m u e", u=2, e=2),
                src.rearrange("p u (m e) -> p m u e", e=2),
                coef_bc[:].unsqueeze(2).unsqueeze(3).to_broadcast([P, P, 2, 2]),
                ALU.mult,
            )

        def quantise_pair(i):
            nc.vector.quantize_mx(
                out=v_codes[:, 2 * i * P:(2 * i + 2) * P].bitcast(FP8X4),
                scales=v_scales[:, 2 * i * P:(2 * i + 2) * P],
                in_=grouped[:, 2 * i:2 * i + 2, :].rearrange("p g c -> p (g c)"),
            )

        scale_group(0)
        scale_group(1)
        for i in range(3):
            scale_group(2 * i + 2)
            quantise_pair(i)
            scale_group(2 * i + 3)
        quantise_pair(3)

        bb = col("bb")
        bz2 = col("bz2", 2)
        zz = col("zz", 2)
        ez = col("ez")
        ezi = col("ezi")
        thz = col("thz")
        cz = col("cz")
        hz = col("hz")
        sc = col("sc")
        g2 = col("g2")
        gw = col("gw")
        nc.scalar.activation(out=t_sb[:], in_=b_bc[:], func=ACT.Square, accum_out=bb[:])
        ts2(bz2[:], bb[:, 0:1].to_broadcast([P, 2]), 1e-15, 400.0, ALU.max, ALU.min)
        nc.gpsimd.tensor_tensor(out=zz[:], in0=bz2[:], in1=pw3[:, 1:3], op=ALU.pow)
        nc.scalar.activation(out=thz[:], in_=zz[:, 0:1], func=ACT.Tanh, scale=0.5)
        nc.scalar.activation(out=ezi[:], in_=zz[:, 0:1], func=ACT.Exp, scale=-1.0)
        nc.scalar.activation(out=ez[:], in_=zz[:, 0:1], func=ACT.Exp)
        tt(hz[:], thz[:], zz[:, 1:2], ALU.mult)
        stt(cz[:], ez[:], 2.0, ezi[:], ALU.add, ALU.add)
        stt(sc[:], cz[:], 0.5, hz[:], ALU.mult, ALU.mult)
        tt(g2[:], sc[:], sc[:], ALU.mult)
        ts2(g2[:], g2[:], bb[:], 1.0, ALU.mult, ALU.add)
        nc.gpsimd.tensor_tensor(out=gw[:], in0=g2[:], in1=pw3[:, 0:1], op=ALU.pow)
        nc.scalar.activation(out=t_sb[:], in_=b_bc[:], func=ACT.Copy, scale=sc[:])

        acc = [None] * BANKS

        def mx_pass(g, j):
            k_off = 4 * (g % 4)
            nc.tensor.matmul_mx(
                out=acc[j][:],
                lhsT=v_codes[:, g * P:(g + 1) * P].bitcast(FP8X4),
                lhsT_scale=v_scales[:, g * P:(g + 1) * P],
                rhs=w[g][:, j * BANK:(j + 1) * BANK].bitcast(FP8X4),
                rhs_scale=planes[g // 4][k_off:P, j * BANK:(j + 1) * BANK],
                start=(g == 0),
                stop=(g == GROUPS - 1),
            )

        s1 = col("s1", BANKS)
        s2 = col("s2", BANKS)

        def dot_t(j):
            nc.vector.scalar_tensor_tensor(
                out=products[j % 4][:], in0=acc[j][:], scalar=1.0, in1=t_sb[:, j * BANK:(j + 1) * BANK],
                op0=ALU.mult, op1=ALU.mult, accum_out=s2[:, j:j + 1],
            )

        last = BANKS - 1
        n2a = col("n2a")
        n2b = col("n2b")
        nb3 = col("nb3", 3)
        d0a = col("d0a")
        for g, j0, j1 in chunks:
            for j in range(j0, j1):
                if g == 0:
                    acc[j] = psum.tile([P, BANK], F32, name="acc%d" % j, tag="bk%d" % j)
                mx_pass(g, j)
            if g == GROUPS - 1:
                for j in range(j0, j1):
                    nc.scalar.activation(out=squares[j % 4][:], in_=acc[j][:], func=ACT.Square, accum_out=s1[:, j:j + 1])
                    if j == last - 1:
                        stt(nb3[:], s1[:, j:j + 1].to_broadcast([P, 3]), n2b[:], cv3[:], ALU.add, ALU.mult)
                        tt(products[j % 4][:], acc[j][:], t_sb[:, j * BANK:(j + 1) * BANK], ALU.mult)
                    elif j < last:
                        dot_t(j)
                    if j == 3:
                        nc.vector.tensor_reduce(out=n2a[:], in_=s1[:, 0:4], axis=AX.X, op=ALU.add)
                        ts1(n2a[:], n2a[:], 1e-12, ALU.max)
                    if j == 5:
                        ts2(n2b[:], n2a[:], s1[:, 4:5], s1[:, 5:6], ALU.add, ALU.add)
                    if j == last:
                        nc.scalar.activation(out=squares[(j + 1) % 4][:], in_=products[(j - 1) % 4][:], func=ACT.Copy,
                                             accum_out=s2[:, j - 1:j])

        nn3 = col("nn3", 3)
        q = col("q")
        dot = col("dot")
        th = col("th")
        er = col("er")
        eri = col("eri")
        eri2 = col("eri2")
        yq = col("yq")
        yqh = col("yqh")
        wq = col("wq")
        c2 = col("c2")
        fac = col("fac")
        stt(nn3[:], cv3[:], s1[:, last:last + 1], nb3[:], ALU.mult, ALU.add)
        nc.gpsimd.tensor_tensor(out=q[:], in0=nn3[:, 0:1], in1=pw3[:, 2:3], op=ALU.pow)
        nc.scalar.activation(out=eri[:], in_=nn3[:, 2:3], func=ACT.Exp, scale=q[:])
        nc.scalar.activation(out=th[:], in_=nn3[:, 1:2], func=ACT.Tanh, scale=q[:])
        nc.scalar.activation(out=er[:], in_=nn3[:, 0:1], func=ACT.Exp, scale=q[:])
        nc.vector.tensor_reduce(out=d0a[:], in_=s2[:, 0:last - 1], axis=AX.X, op=ALU.add)
        dot_t(last)
        ts2(dot[:], s2[:, last:last + 1], s2[:, last - 1:last], d0a[:], ALU.add, ALU.add)
        ts1(eri2[:], eri[:], 2.0, ALU.add)
        tt(yq[:], th[:], q[:], ALU.mult)
        stt(yqh[:], th[:], 0.5, q[:], ALU.mult, ALU.mult)
        ts2(wq[:], yq[:], dot[:], gw[:], ALU.mult, ALU.add)
        stt(c2[:], er[:], math.e ** 20.0, eri2[:], ALU.min, ALU.add)
        stt(fac[:], c2[:], yqh[:], wq[:], ALU.mult, ALU.mult)

        for j in range(BANKS):
            cols = slice(j * BANK, (j + 1) * BANK)
            stt(o_sb[:, cols], acc[j][:], fac[:], t_sb[:, cols], ALU.mult, ALU.add)
            nc.sync.dma_start(out=out[:, cols], in_=o_sb[:, cols])
